import numpy as np
import ml_dtypes

BF16 = ml_dtypes.bfloat16


def bf(x):
    return np.asarray(x, np.float32).astype(BF16)


def f32(x):
    return np.asarray(x, np.float32)


def f64(x):
    return np.asarray(x).astype(np.float64)


def striped(idx):
    return np.tile(idx.reshape(-1, 16).T, (8, 1))


C, S, N, T, B = 512, 4096, 8192, 8, 1024


def posenc():
    pos = np.arange(T, dtype=np.float64)[None, :]
    div = np.exp(np.arange(0, C, 2, dtype=np.float64) * (-np.log(10000.0) / C))[:, None]
    pe = np.zeros((C, T))
    pe[0::2] = np.sin(div * pos)
    pe[1::2] = np.cos(div * pos)
    return pe


def setup_inputs():
    return {"table": f32(np.random.standard_normal((C, S))), "pe": f32(posenc()), "offs": striped(np.concatenate([np.random.permutation(S) for _ in range(N // S)]))}


def reference(table, pe, offs):
    idx = offs[:16].T.reshape(-1)
    h = f64(table)[:, idx].reshape(C, B, T) + f64(pe)[:, None, :]
    return h.max(axis=2)

@@ -1,0 +1,52 @@
+import concourse.mybir as mybir
+
+F32 = mybir.dt.float32
+U16 = mybir.dt.uint16
+
+P = 128
+C = 512
+S = 4096
+N = 8192
+T = 8
+BLOCKS = C // P
+PIECE = 4096
+PIECES = N // PIECE
+SEQS = PIECE // T
+
+
+def tile_selfattention3_kernel(tc, table, pe, offs, out):
+    nc = tc.nc
+    with (
+        tc.tile_pool(name="held", bufs=1) as held,
+        tc.tile_pool(name="work", bufs=2) as work,
+    ):
+        offsets = held.tile([P, N // 16], U16, name="offsets")
+        nc.sync.dma_start(offsets[:], offs)
+
+        pe_all = held.tile([P, BLOCKS, T], F32, name="pe_all")
+        nc.scalar.dma_start(pe_all[:], pe.rearrange("(k p) t -> p k t", p=P))
+
+        windows = []
+        for k in range(BLOCKS):
+            window = held.tile([P, S], F32, name=f"window{k}")
+            nc.sync.dma_start(window[:], table[k * P : (k + 1) * P, :])
+            windows.append(window)
+
+        for k in range(BLOCKS):
+            pe_repeated = held.tile([P, SEQS, T], F32, name=f"pe_repeated{k}")
+            nc.scalar.copy(pe_repeated[:], pe_all[:, k : k + 1, :].to_broadcast([P, SEQS, T]))
+            for i in range(PIECES):
+                tokens = work.tile([P, SEQS, T], F32, name="tokens")
+                nc.vector.tensor_tensor(
+                    tokens[:],
+                    windows[k][:].indirect(offsets[:, i * (PIECE // 16) : (i + 1) * (PIECE // 16)]),
+                    pe_repeated[:],
+                    mybir.AluOpType.add,
+                )
+                pooled = work.tile([P, SEQS], F32, name="pooled")
+                nc.vector.tensor_reduce(
+                    pooled[:], tokens[:], mybir.AxisListType.X, mybir.AluOpType.max
+                )
+                nc.scalar.dma_start(
+                    out[k * P : (k + 1) * P, i * SEQS : (i + 1) * SEQS], pooled[:]
+                )

@@ -43,10 +43,17 @@ def tile_selfattention3_kernel(tc, table, pe, offs, out):
                     pe_repeated[:],
                     mybir.AluOpType.add,
                 )
-                pooled = work.tile([P, SEQS], F32, name="pooled")
-                nc.vector.tensor_reduce(
-                    pooled[:], tokens[:], mybir.AxisListType.X, mybir.AluOpType.max
-                )
+                best = tokens
+                for width in (T // 2, T // 4, T // 8):
+                    halved = work.tile([P, SEQS, width], F32, name=f"best{width}")
+                    nc.vector.tensor_tensor(
+                        halved[:],
+                        best[:, :, 0:width],
+                        best[:, :, width : 2 * width],
+                        mybir.AluOpType.max,
+                    )
+                    best = halved
                 nc.scalar.dma_start(
-                    out[k * P : (k + 1) * P, i * SEQS : (i + 1) * SEQS], pooled[:]
+                    out[k * P : (k + 1) * P, i * SEQS : (i + 1) * SEQS],
+                    best[:].rearrange("p b t -> p (b t)"),
                 )

@@ -20,21 +20,25 @@ def tile_selfattention3_kernel(tc, table, pe, offs, out):
         tc.tile_pool(name="held", bufs=1) as held,
         tc.tile_pool(name="work", bufs=2) as work,
     ):
+        windows = []
+        for k in range(BLOCKS):
+            window = held.tile([P, S], F32, name=f"window{k}")
+            nc.scalar.dma_start(window[:], table[k * P : (k + 1) * P, :])
+            windows.append(window)
+
         offsets = held.tile([P, N // 16], U16, name="offsets")
         nc.sync.dma_start(offsets[:], offs)
 
         pe_all = held.tile([P, BLOCKS, T], F32, name="pe_all")
-        nc.scalar.dma_start(pe_all[:], pe.rearrange("(k p) t -> p k t", p=P))
-
-        windows = []
-        for k in range(BLOCKS):
-            window = held.tile([P, S], F32, name=f"window{k}")
-            nc.sync.dma_start(window[:], table[k * P : (k + 1) * P, :])
-            windows.append(window)
+        nc.sync.dma_start(pe_all[:], pe.rearrange("(k p) t -> p k t", p=P))
 
         for k in range(BLOCKS):
             pe_repeated = held.tile([P, SEQS, T], F32, name=f"pe_repeated{k}")
-            nc.scalar.copy(pe_repeated[:], pe_all[:, k : k + 1, :].to_broadcast([P, SEQS, T]))
+            pe_of_block = pe_all[:, k : k + 1, :].to_broadcast([P, SEQS, T])
+            if k == 0:
+                nc.vector.tensor_copy(pe_repeated[:], pe_of_block)
+            else:
+                nc.scalar.copy(pe_repeated[:], pe_of_block)
             for i in range(PIECES):
                 tokens = work.tile([P, SEQS, T], F32, name="tokens")
                 nc.vector.tensor_tensor(
@@ -53,7 +57,7 @@ def tile_selfattention3_kernel(tc, table, pe, offs, out):
                         mybir.AluOpType.max,
                     )
                     best = halved
-                nc.scalar.dma_start(
+                nc.sync.dma_start(
                     out[k * P : (k + 1) * P, i * SEQS : (i + 1) * SEQS],
                     best[:].rearrange("p b t -> p (b t)"),
                 )

@@ -8,6 +8,7 @@ C = 512
 S = 4096
 N = 8192
 T = 8
+B = N // T
 BLOCKS = C // P
 PIECE = 4096
 PIECES = N // PIECE
@@ -20,44 +21,41 @@ def tile_selfattention3_kernel(tc, table, pe, offs, out):
         tc.tile_pool(name="held", bufs=1) as held,
         tc.tile_pool(name="work", bufs=2) as work,
     ):
-        windows = []
-        for k in range(BLOCKS):
-            window = held.tile([P, S], F32, name=f"window{k}")
-            nc.scalar.dma_start(window[:], table[k * P : (k + 1) * P, :])
-            windows.append(window)
-
         offsets = held.tile([P, N // 16], U16, name="offsets")
         nc.sync.dma_start(offsets[:], offs)
 
         pe_all = held.tile([P, BLOCKS, T], F32, name="pe_all")
-        nc.sync.dma_start(pe_all[:], pe.rearrange("(k p) t -> p k t", p=P))
+        nc.scalar.dma_start(pe_all[:], pe.rearrange("(k p) t -> p k t", p=P))
+
+        windows = []
+        for k in range(BLOCKS):
+            window = held.tile([P, S], F32, name=f"window{k}")
+            nc.sync.dma_start(window[:], table[k * P : (k + 1) * P, :])
+            windows.append(window)
 
         for k in range(BLOCKS):
-            pe_repeated = held.tile([P, SEQS, T], F32, name=f"pe_repeated{k}")
-            pe_of_block = pe_all[:, k : k + 1, :].to_broadcast([P, SEQS, T])
-            if k == 0:
-                nc.vector.tensor_copy(pe_repeated[:], pe_of_block)
-            else:
-                nc.scalar.copy(pe_repeated[:], pe_of_block)
+            pe_repeated = work.tile([P, SEQS, T], F32, name="pe_repeated")
+            nc.scalar.copy(pe_repeated[:], pe_all[:, k : k + 1, :].to_broadcast([P, SEQS, T]))
+
+            tokens = work.tile([P, B, T], F32, name="tokens")
             for i in range(PIECES):
-                tokens = work.tile([P, SEQS, T], F32, name="tokens")
                 nc.vector.tensor_tensor(
-                    tokens[:],
+                    tokens[:, i * SEQS : (i + 1) * SEQS, :],
                     windows[k][:].indirect(offsets[:, i * (PIECE // 16) : (i + 1) * (PIECE // 16)]),
                     pe_repeated[:],
                     mybir.AluOpType.add,
                 )
-                best = tokens
-                for width in (T // 2, T // 4, T // 8):
-                    halved = work.tile([P, SEQS, width], F32, name=f"best{width}")
-                    nc.vector.tensor_tensor(
-                        halved[:],
-                        best[:, :, 0:width],
-                        best[:, :, width : 2 * width],
-                        mybir.AluOpType.max,
-                    )
-                    best = halved
-                nc.sync.dma_start(
-                    out[k * P : (k + 1) * P, i * SEQS : (i + 1) * SEQS],
-                    best[:].rearrange("p b t -> p (b t)"),
+
+            best = tokens
+            for width in (T // 2, T // 4, T // 8):
+                halved = work.tile([P, B, width], F32, name=f"best{width}")
+                nc.vector.tensor_tensor(
+                    halved[:],
+                    best[:, :, 0:width],
+                    best[:, :, width : 2 * width],
+                    mybir.AluOpType.max,
                 )
+                best = halved
+            nc.scalar.dma_start(
+                out[k * P : (k + 1) * P, :], best[:].rearrange("p b t -> p (b t)")
+            )

@@ -8,7 +8,6 @@ C = 512
 S = 4096
 N = 8192
 T = 8
-B = N // T
 BLOCKS = C // P
 PIECE = 4096
 PIECES = N // PIECE
@@ -34,28 +33,31 @@ def tile_selfattention3_kernel(tc, table, pe, offs, out):
             windows.append(window)
 
         for k in range(BLOCKS):
-            pe_repeated = work.tile([P, SEQS, T], F32, name="pe_repeated")
-            nc.scalar.copy(pe_repeated[:], pe_all[:, k : k + 1, :].to_broadcast([P, SEQS, T]))
-
-            tokens = work.tile([P, B, T], F32, name="tokens")
+            pe_repeated = held.tile([P, SEQS, T], F32, name=f"pe_repeated{k}")
+            pe_of_block = pe_all[:, k : k + 1, :].to_broadcast([P, SEQS, T])
+            if k == 0:
+                nc.vector.tensor_copy(pe_repeated[:], pe_of_block)
+            else:
+                nc.scalar.copy(pe_repeated[:], pe_of_block)
             for i in range(PIECES):
+                tokens = work.tile([P, SEQS, T], F32, name="tokens")
                 nc.vector.tensor_tensor(
-                    tokens[:, i * SEQS : (i + 1) * SEQS, :],
+                    tokens[:],
                     windows[k][:].indirect(offsets[:, i * (PIECE // 16) : (i + 1) * (PIECE // 16)]),
                     pe_repeated[:],
                     mybir.AluOpType.add,
                 )
-
-            best = tokens
-            for width in (T // 2, T // 4, T // 8):
-                halved = work.tile([P, B, width], F32, name=f"best{width}")
-                nc.vector.tensor_tensor(
-                    halved[:],
-                    best[:, :, 0:width],
-                    best[:, :, width : 2 * width],
-                    mybir.AluOpType.max,
+                best = tokens
+                for width in (T // 2, T // 4, T // 8):
+                    halved = work.tile([P, SEQS, width], F32, name=f"best{width}")
+                    nc.vector.tensor_tensor(
+                        halved[:],
+                        best[:, :, 0:width],
+                        best[:, :, width : 2 * width],
+                        mybir.AluOpType.max,
+                    )
+                    best = halved
+                nc.scalar.dma_start(
+                    out[k * P : (k + 1) * P, i * SEQS : (i + 1) * SEQS],
+                    best[:].rearrange("p b t -> p (b t)"),
                 )
-                best = halved
-            nc.scalar.dma_start(
-                out[k * P : (k + 1) * P, :], best[:].rearrange("p b t -> p (b t)")
-            )

import concourse.mybir as mybir

F32 = mybir.dt.float32
U16 = mybir.dt.uint16

P = 128
C = 512
S = 4096
N = 8192
T = 8
BLOCKS = C // P
PIECE = 4096
PIECES = N // PIECE
SEQS = PIECE // T


def tile_selfattention3_kernel(tc, table, pe, offs, out):
    nc = tc.nc
    with (
        tc.tile_pool(name="held", bufs=1) as held,
        tc.tile_pool(name="work", bufs=2) as work,
    ):
        offsets = held.tile([P, N // 16], U16, name="offsets")
        nc.sync.dma_start(offsets[:], offs)

        pe_all = held.tile([P, BLOCKS, T], F32, name="pe_all")
        nc.scalar.dma_start(pe_all[:], pe.rearrange("(k p) t -> p k t", p=P))

        windows = []
        for k in range(BLOCKS):
            window = held.tile([P, S], F32, name=f"window{k}")
            nc.sync.dma_start(window[:], table[k * P : (k + 1) * P, :])
            windows.append(window)

        for k in range(BLOCKS):
            pe_repeated = held.tile([P, SEQS, T], F32, name=f"pe_repeated{k}")
            pe_of_block = pe_all[:, k : k + 1, :].to_broadcast([P, SEQS, T])
            if k == 0:
                nc.vector.tensor_copy(pe_repeated[:], pe_of_block)
            else:
                nc.scalar.copy(pe_repeated[:], pe_of_block)
            for i in range(PIECES):
                tokens = work.tile([P, SEQS, T], F32, name="tokens")
                nc.vector.tensor_tensor(
                    tokens[:],
                    windows[k][:].indirect(offsets[:, i * (PIECE // 16) : (i + 1) * (PIECE // 16)]),
                    pe_repeated[:],
                    mybir.AluOpType.add,
                )
                best = tokens
                for width in (T // 2, T // 4, T // 8):
                    halved = work.tile([P, SEQS, width], F32, name=f"best{width}")
                    nc.vector.tensor_tensor(
                        halved[:],
                        best[:, :, 0:width],
                        best[:, :, width : 2 * width],
                        mybir.AluOpType.max,
                    )
                    best = halved
                nc.scalar.dma_start(
                    out[k * P : (k + 1) * P, i * SEQS : (i + 1) * SEQS],
                    best[:].rearrange("p b t -> p (b t)"),
                )
